import numpy as np
import ml_dtypes


def mxq(x, axis, fmt="e4m3"):
    dtype, down = {"e4m3": (ml_dtypes.float8_e4m3fn, 7), "e5m2": (ml_dtypes.float8_e5m2, 14)}[fmt]
    v = np.moveaxis(np.asarray(x, np.float32).astype(ml_dtypes.bfloat16).astype(np.float64), axis, -1)
    blocks = v.reshape(v.shape[:-1] + (-1, 32))
    amax = np.abs(blocks).max(-1, keepdims=True)
    byte = np.maximum(np.where(amax > 0, np.frexp(amax)[1] - 1 + 127, 0) - down, 1)
    scale = np.exp2(byte - 127.0)
    codes = (blocks / scale).astype(np.float32).astype(dtype).astype(np.float64)
    return np.moveaxis((codes * scale).reshape(v.shape), -1, axis)


WIDE = False


def mx_kscale(k):
    if not WIDE:
        return np.ones(k)
    levels = np.array([10, -10, 5, -5, 0])
    a = np.random.permutation(np.resize(levels, k // 512 * 4)).reshape(k // 512, 4)
    idx = np.arange(k)
    return np.exp2(a[idx // 512, idx % 128 // 32])


BF16 = ml_dtypes.bfloat16


def bf(x):
    return np.asarray(x, np.float32).astype(BF16)


def f64(x):
    return np.asarray(x).astype(np.float64)


E2M1 = np.array([0.0, 0.5, 1.0, 1.5, 2.0, 3.0, 4.0, 6.0, -0.0, -0.5, -1.0, -1.5, -2.0, -3.0, -4.0, -6.0])


def pack_weight(w, fmt):
    k, n = w.shape
    w = f64(bf(w)).reshape(k // 32, 32, n)
    amax = np.abs(w).max(1)
    if fmt == "e4m3":
        byte = np.frexp(amax)[1] - 1 + 127 - 7
    else:
        mant, ex = np.frexp(amax / 6.0)
        byte = np.where(mant > 0.5, ex, ex - 1) + 127
    byte = np.clip(np.where(amax > 0, byte, 1), 1, 254)
    scaled = (w * np.exp2(127.0 - byte)[:, None, :]).reshape(k, n).astype(np.float32)
    by_word = np.ascontiguousarray(scaled.reshape(k // 512, 128, 4, n).transpose(0, 1, 3, 2))
    if fmt == "e4m3":
        words = by_word.astype(ml_dtypes.float8_e4m3fn).view(np.uint8)
    else:
        c = by_word.astype(ml_dtypes.float4_e2m1fn).view(np.uint8) & 0xF
        words = c[..., 0::2] | (c[..., 1::2] << 4)
    return np.ascontiguousarray(words), np.ascontiguousarray(byte.astype(np.uint8).reshape(k // 512, 16, n))


def unpack_weight(words, scales, fmt):
    g, p, n, _ = words.shape
    if fmt == "e4m3":
        vals = np.ascontiguousarray(words).view(ml_dtypes.float8_e4m3fn).astype(np.float64)
    else:
        nib = np.empty((g, p, n, 4), np.uint8)
        nib[..., 0::2] = words & 0xF
        nib[..., 1::2] = words >> 4
        vals = E2M1[nib]
    vals = vals * np.repeat(np.exp2(scales.astype(np.float64) - 127.0), 8, axis=1)[..., None]
    return vals.transpose(0, 1, 3, 2).reshape(g * 512, n)


I, H, B = 2048, 2048, 128
FMT = "e4m3"


def sigmoid(v):
    return 1.0 / (1.0 + np.exp(-v))


def setup_inputs():
    s, t = mx_kscale(I), mx_kscale(H)
    d = {"x": bf(np.random.standard_normal((I, B)) * s[:, None]), "h": bf(np.random.standard_normal((B, H)) * t[None, :]),
         "c": bf(np.random.standard_normal((B, H))), "ig": bf(np.random.standard_normal((H, B)) * 0.35)}
    for n in ("w_if", "w_io"):
        w = np.random.standard_normal((H, I)) * 0.7 / np.sqrt(I) / s[None, :]
        d[n + "_words"], d[n + "_scales"] = pack_weight(np.ascontiguousarray(w.T), FMT)
    for n in ("w_hf", "w_ho"):
        w = np.random.standard_normal((H, H)) * 0.7 / np.sqrt(H) / t[None, :]
        d[n + "_words"], d[n + "_scales"] = pack_weight(np.ascontiguousarray(w.T), FMT)
    for n in ("b_if", "b_hf", "b_io", "b_ho"):
        d[n] = bf(np.random.standard_normal((H, 1)) * 0.3)
    return d


def reference(x, h, c, ig, w_if_words, w_if_scales, w_io_words, w_io_scales, w_hf_words, w_hf_scales, w_ho_words, w_ho_scales, b_if, b_hf, b_io, b_ho):
    xq = mxq(f64(x), 0, "e4m3")
    hq = mxq(f64(h).T, 0, "e4m3")
    f = sigmoid((unpack_weight(w_if_words, w_if_scales, FMT).T @ xq) + f64(b_if) + (unpack_weight(w_hf_words, w_hf_scales, FMT).T @ hq) + f64(b_hf))
    o = sigmoid((unpack_weight(w_io_words, w_io_scales, FMT).T @ xq) + f64(b_io) + (unpack_weight(w_ho_words, w_ho_scales, FMT).T @ hq) + f64(b_ho))
    c_next_t = f * f64(c).T + f64(ig)
    h_next_t = o * np.tanh(c_next_t)
    return h_next_t.T, c_next_t.T

@@ -1,0 +1,216 @@
+import concourse.mybir as mybir
+from concourse.masks import make_identity
+
+F32 = mybir.dt.float32
+BF16 = mybir.dt.bfloat16
+I32 = mybir.dt.int32
+U32 = mybir.dt.uint32
+U8 = mybir.dt.uint8
+FP8X4 = mybir.dt.float8_e4m3fn_x4
+ADD = mybir.AluOpType.add
+MULT = mybir.AluOpType.mult
+SIGMOID = mybir.ActivationFunctionType.Sigmoid
+TANH = mybir.ActivationFunctionType.Tanh
+
+P = 128
+PACK = 4
+K_PASS = P * PACK
+FEATURES = 2048
+PASSES = FEATURES // K_PASS
+N_TILE = 512
+CHUNKS = FEATURES // N_TILE
+QUADRANT = 32
+ROWS = 4
+
+FLOPS = 4 * 2 * FEATURES * FEATURES * P
+
+
+def chunk(j):
+    return slice(j * N_TILE, (j + 1) * N_TILE)
+
+
+def load_words(nc, pool, name, words):
+    tiles = []
+    for g in range(PASSES):
+        tile_g = pool.tile([P, FEATURES], U32, name="%s_words_%d" % (name, g), align_bytes=64)
+        nc.sync.dma_start(
+            out=tile_g[:].bitcast(I32),
+            in_=words[g].rearrange("p n t -> p (n t)").bitcast(I32),
+        )
+        tiles.append(tile_g)
+    return tiles
+
+
+def load_scale_planes(nc, planes, scales):
+    for quadrant in range(P // QUADRANT):
+        first = quadrant * QUADRANT
+        nc.sync.dma_start(
+            out=planes[first : first + PASSES * ROWS, :].bitcast(I32),
+            in_=scales[:, quadrant * ROWS : (quadrant + 1) * ROWS, :].bitcast(I32),
+        )
+
+
+def tile_naivelstm_pb_kernel(
+    tc,
+    x,
+    h,
+    c,
+    ig,
+    w_if_words,
+    w_if_scales,
+    w_io_words,
+    w_io_scales,
+    w_hf_words,
+    w_hf_scales,
+    w_ho_words,
+    w_ho_scales,
+    b_if,
+    b_hf,
+    b_io,
+    b_ho,
+    out_0,
+    out_1,
+):
+    nc = tc.nc
+    with (
+        tc.tile_pool(name="keep", bufs=1) as keep,
+        tc.tile_pool(name="work", bufs=3) as work,
+        tc.tile_pool(name="result", bufs=CHUNKS) as result,
+        tc.psum_pool(name="psum", bufs=8) as psum,
+    ):
+        planes = {}
+        for name in ("if", "hf", "io", "ho"):
+            planes[name] = keep.tile([P, FEATURES], U8, name="%s_planes" % name, align_bytes=64)
+            nc.vector.memset(planes[name][:].bitcast(I32), 0)
+        bias_rows = keep.tile([P, 2, FEATURES], BF16)
+        nc.vector.memset(bias_rows[:], 0.0)
+        ones = keep.tile([P, P], BF16)
+        nc.vector.memset(ones[:], 1.0)
+        ident_f32 = keep.tile([P, P], F32)
+        make_identity(nc, ident_f32[:])
+        ident_bf16 = keep.tile([P, P], BF16)
+        make_identity(nc, ident_bf16[:])
+
+        x_raw = keep.tile([P, PASSES, PACK, P], BF16)
+        nc.sync.dma_start(out=x_raw[:], in_=x.rearrange("(g p t) b -> p g t b", p=P, t=PACK))
+        h_raw = keep.tile([P, FEATURES], BF16)
+        nc.sync.dma_start(out=h_raw[:], in_=h)
+        for gate, (b_x, b_h) in enumerate(((b_if, b_hf), (b_io, b_ho))):
+            nc.sync.dma_start(out=bias_rows[0:1, gate, :], in_=b_x.rearrange("n o -> o n"))
+            nc.sync.dma_start(out=bias_rows[1:2, gate, :], in_=b_h.rearrange("n o -> o n"))
+        ig_raw = keep.tile([P, CHUNKS, PACK, P], BF16)
+        nc.sync.dma_start(out=ig_raw[:], in_=ig.rearrange("(j p t) b -> p j t b", p=P, t=PACK))
+        load_scale_planes(nc, planes["if"], w_if_scales)
+        load_scale_planes(nc, planes["hf"], w_hf_scales)
+        load_scale_planes(nc, planes["io"], w_io_scales)
+        load_scale_planes(nc, planes["ho"], w_ho_scales)
+        c_sb = keep.tile([P, FEATURES], BF16)
+        nc.sync.dma_start(out=c_sb[:], in_=c)
+        words = {}
+        words["if"] = load_words(nc, keep, "if", w_if_words)
+        words["hf"] = load_words(nc, keep, "hf", w_hf_words)
+        words["io"] = load_words(nc, keep, "io", w_io_words)
+        words["ho"] = load_words(nc, keep, "ho", w_ho_words)
+
+        x_grouped = keep.tile([P, PASSES, P, PACK], BF16, align_bytes=64)
+        nc.vector.tensor_copy(out=x_grouped[:], in_=x_raw[:].rearrange("p g t b -> p g b t"))
+        x_codes = keep.tile([P, PASSES, P], U32, align_bytes=64)
+        x_scales = keep.tile([P, PASSES, P], U8, align_bytes=64)
+        nc.vector.quantize_mx(
+            out=x_codes[:].rearrange("p g b -> p (g b)").bitcast(FP8X4),
+            scales=x_scales[:].rearrange("p g b -> p (g b)"),
+            in_=x_grouped[:].rearrange("p g b t -> p (g b t)"),
+        )
+
+        h_words = h_raw[:].bitcast(F32)
+        h_grouped = keep.tile([P, PASSES, P, 2], F32, align_bytes=64)
+        for half in range(2):
+            h_t = psum.tile([P, 2, 2, P], F32, tag="bank")
+            for gg in range(2):
+                g = 2 * half + gg
+                for u in range(2):
+                    nc.tensor.transpose(
+                        h_t[:, gg, u, :],
+                        h_words[:, 256 * g + u : 256 * (g + 1) : 2],
+                        ident_f32[:],
+                    )
+            nc.vector.tensor_copy(
+                out=h_grouped[:, 2 * half : 2 * half + 2, :, :],
+                in_=h_t[:].rearrange("p g u b -> p g b u"),
+            )
+        h_codes = keep.tile([P, PASSES, P], U32, align_bytes=64)
+        h_scales = keep.tile([P, PASSES, P], U8, align_bytes=64)
+        nc.vector.quantize_mx(
+            out=h_codes[:].rearrange("p g b -> p (g b)").bitcast(FP8X4),
+            scales=h_scales[:].rearrange("p g b -> p (g b)"),
+            in_=h_grouped[:].rearrange("p g b u -> p (g b u)").bitcast(BF16),
+        )
+
+        ig_t = keep.tile([P, CHUNKS, P, PACK], BF16)
+        for half in range(2):
+            ig_bank = psum.tile([P, 2, PACK, P], BF16, tag="bank")
+            for jj in range(2):
+                for t in range(PACK):
+                    nc.tensor.transpose(
+                        ig_bank[:, jj, t, :], ig_raw[:, 2 * half + jj, t, :], ident_bf16[:]
+                    )
+            nc.vector.tensor_copy(
+                out=ig_t[:, 2 * half : 2 * half + 2, :, :],
+                in_=ig_bank[:].rearrange("b j t p -> b j p t"),
+            )
+        ig_rows = ig_t[:].rearrange("b j p t -> b (j p t)")
+
+        bias_all = keep.tile([P, 2, FEATURES], F32)
+        for gate in range(2):
+            for j in range(CHUNKS):
+                bias_bank = psum.tile([P, N_TILE], F32, tag="bank")
+                nc.tensor.matmul(
+                    out=bias_bank[:], lhsT=ones[:], rhs=bias_rows[:, gate, chunk(j)],
+                    start=True, stop=True,
+                )
+                nc.scalar.copy(out=bias_all[:, gate, chunk(j)], in_=bias_bank[:])
+
+        def gate_sums(gate_name, x_weight, h_weight):
+            banks = [
+                psum.tile([P, N_TILE], F32, tag="bank", name="%s_bank_%d" % (gate_name, j))
+                for j in range(CHUNKS)
+            ]
+            sides = ((x_codes, x_scales, x_weight), (h_codes, h_scales, h_weight))
+            for side, (codes, scales, weight) in enumerate(sides):
+                for g in range(PASSES):
+                    for j in range(CHUNKS):
+                        nc.tensor.matmul_mx(
+                            out=banks[j][:],
+                            lhsT=codes[:, g, :].bitcast(FP8X4),
+                            lhsT_scale=scales[:, g, :],
+                            rhs=words[weight][g][:, chunk(j)].bitcast(FP8X4),
+                            rhs_scale=planes[weight][ROWS * g : P, chunk(j)],
+                            start=(side == 0 and g == 0),
+                            stop=(side == 1 and g == PASSES - 1),
+                        )
+            return banks
+
+        def gate_value(bank, gate, j):
+            value = work.tile([P, N_TILE], F32, tag="gate")
+            nc.vector.tensor_tensor(out=value[:], in0=bank[:], in1=bias_all[:, gate, chunk(j)], op=ADD)
+            nc.scalar.activation(out=value[:], in_=value[:], func=SIGMOID)
+            return value
+
+        f_banks = gate_sums("f", "if", "hf")
+        c_next = keep.tile([P, FEATURES], F32)
+        tanh_c = keep.tile([P, FEATURES], F32)
+        for j in range(CHUNKS):
+            f_gate = gate_value(f_banks[j], 0, j)
+            nc.vector.tensor_tensor(out=c_next[:, chunk(j)], in0=f_gate[:], in1=c_sb[:, chunk(j)], op=MULT)
+            nc.vector.tensor_tensor(
+                out=c_next[:, chunk(j)], in0=c_next[:, chunk(j)], in1=ig_rows[:, chunk(j)], op=ADD
+            )
+            nc.scalar.activation(out=tanh_c[:, chunk(j)], in_=c_next[:, chunk(j)], func=TANH)
+        nc.sync.dma_start(out=out_1, in_=c_next[:])
+
+        o_banks = gate_sums("o", "io", "ho")
+        for j in range(CHUNKS):
+            o_gate = gate_value(o_banks[j], 1, j)
+            h_next = result.tile([P, N_TILE], F32)
+            nc.vector.tensor_tensor(out=h_next[:], in0=o_gate[:], in1=tanh_c[:, chunk(j)], op=MULT)
+            nc.sync.dma_start(out=out_0[:, chunk(j)], in_=h_next[:])

@@ -44,9 +44,9 @@ def load_words(nc, pool, name, words):
 def load_scale_planes(nc, planes, scales):
     for quadrant in range(P // QUADRANT):
         first = quadrant * QUADRANT
-        nc.sync.dma_start(
-            out=planes[first : first + PASSES * ROWS, :].bitcast(I32),
-            in_=scales[:, quadrant * ROWS : (quadrant + 1) * ROWS, :].bitcast(I32),
+        nc.gpsimd.dma_start(
+            out=planes[first : first + PASSES * ROWS, :].bitcast(F32),
+            in_=scales[:, quadrant * ROWS : (quadrant + 1) * ROWS, :].bitcast(F32),
         )
 
 
@@ -96,8 +96,8 @@ def tile_naivelstm_pb_kernel(
         h_raw = keep.tile([P, FEATURES], BF16)
         nc.sync.dma_start(out=h_raw[:], in_=h)
         for gate, (b_x, b_h) in enumerate(((b_if, b_hf), (b_io, b_ho))):
-            nc.sync.dma_start(out=bias_rows[0:1, gate, :], in_=b_x.rearrange("n o -> o n"))
-            nc.sync.dma_start(out=bias_rows[1:2, gate, :], in_=b_h.rearrange("n o -> o n"))
+            nc.scalar.dma_start(out=bias_rows[0:1, gate, :], in_=b_x.rearrange("n o -> o n"))
+            nc.scalar.dma_start(out=bias_rows[1:2, gate, :], in_=b_h.rearrange("n o -> o n"))
         ig_raw = keep.tile([P, CHUNKS, PACK, P], BF16)
         nc.sync.dma_start(out=ig_raw[:], in_=ig.rearrange("(j p t) b -> p j t b", p=P, t=PACK))
         load_scale_planes(nc, planes["if"], w_if_scales)

@@ -21,6 +21,7 @@ N_TILE = 512
 CHUNKS = FEATURES // N_TILE
 QUADRANT = 32
 ROWS = 4
+LATE_PASSES = 2
 
 FLOPS = 4 * 2 * FEATURES * FEATURES * P
 
@@ -29,16 +30,18 @@ def chunk(j):
     return slice(j * N_TILE, (j + 1) * N_TILE)
 
 
-def load_words(nc, pool, name, words):
-    tiles = []
-    for g in range(PASSES):
-        tile_g = pool.tile([P, FEATURES], U32, name="%s_words_%d" % (name, g), align_bytes=64)
-        nc.sync.dma_start(
-            out=tile_g[:].bitcast(I32),
-            in_=words[g].rearrange("p n t -> p (n t)").bitcast(I32),
-        )
-        tiles.append(tile_g)
-    return tiles
+def words_tiles(pool, name):
+    return [
+        pool.tile([P, FEATURES], U32, name="%s_words_%d" % (name, g), align_bytes=64)
+        for g in range(PASSES)
+    ]
+
+
+def load_words(nc, tile_g, words_g, columns):
+    nc.sync.dma_start(
+        out=tile_g[:, columns].bitcast(I32),
+        in_=words_g.rearrange("p n t -> p (n t)").bitcast(I32)[:, columns],
+    )
 
 
 def load_scale_planes(nc, planes, scales):
@@ -107,10 +110,16 @@ def tile_naivelstm_pb_kernel(
         c_sb = keep.tile([P, FEATURES], BF16)
         nc.sync.dma_start(out=c_sb[:], in_=c)
         words = {}
-        words["if"] = load_words(nc, keep, "if", w_if_words)
-        words["hf"] = load_words(nc, keep, "hf", w_hf_words)
-        words["io"] = load_words(nc, keep, "io", w_io_words)
-        words["ho"] = load_words(nc, keep, "ho", w_ho_words)
+        for name in ("if", "hf", "io", "ho"):
+            words[name] = words_tiles(keep, name)
+        for name, dram in (("if", w_if_words), ("hf", w_hf_words), ("io", w_io_words)):
+            for g in range(PASSES):
+                load_words(nc, words[name][g], dram[g], slice(0, FEATURES))
+        for g in range(PASSES - LATE_PASSES):
+            load_words(nc, words["ho"][g], w_ho_words[g], slice(0, FEATURES))
+        for j in range(CHUNKS):
+            for g in range(PASSES - LATE_PASSES, PASSES):
+                load_words(nc, words["ho"][g], w_ho_words[g], chunk(j))
 
         x_grouped = keep.tile([P, PASSES, P, PACK], BF16, align_bytes=64)
         nc.vector.tensor_copy(out=x_grouped[:], in_=x_raw[:].rearrange("p g t b -> p g b t"))
@@ -170,25 +179,33 @@ def tile_naivelstm_pb_kernel(
                 )
                 nc.scalar.copy(out=bias_all[:, gate, chunk(j)], in_=bias_bank[:])
 
-        def gate_sums(gate_name, x_weight, h_weight):
+        def mx_pass(bank, j, codes, scales, weight, g, start, stop):
+            nc.tensor.matmul_mx(
+                out=bank[:],
+                lhsT=codes[:, g, :].bitcast(FP8X4),
+                lhsT_scale=scales[:, g, :],
+                rhs=words[weight][g][:, chunk(j)].bitcast(FP8X4),
+                rhs_scale=planes[weight][ROWS * g : P, chunk(j)],
+                start=start,
+                stop=stop,
+            )
+
+        def open_banks(gate_name, x_weight, h_weight):
             banks = [
                 psum.tile([P, N_TILE], F32, tag="bank", name="%s_bank_%d" % (gate_name, j))
                 for j in range(CHUNKS)
             ]
-            sides = ((x_codes, x_scales, x_weight), (h_codes, h_scales, h_weight))
-            for side, (codes, scales, weight) in enumerate(sides):
-                for g in range(PASSES):
-                    for j in range(CHUNKS):
-                        nc.tensor.matmul_mx(
-                            out=banks[j][:],
-                            lhsT=codes[:, g, :].bitcast(FP8X4),
-                            lhsT_scale=scales[:, g, :],
-                            rhs=words[weight][g][:, chunk(j)].bitcast(FP8X4),
-                            rhs_scale=planes[weight][ROWS * g : P, chunk(j)],
-                            start=(side == 0 and g == 0),
-                            stop=(side == 1 and g == PASSES - 1),
-                        )
+            for g in range(PASSES):
+                for j in range(CHUNKS):
+                    mx_pass(banks[j], j, x_codes, x_scales, x_weight, g, g == 0, False)
+            for g in range(PASSES - LATE_PASSES):
+                for j in range(CHUNKS):
+                    mx_pass(banks[j], j, h_codes, h_scales, h_weight, g, False, False)
             return banks
+
+        def close_bank(bank, j, h_weight):
+            for g in range(PASSES - LATE_PASSES, PASSES):
+                mx_pass(bank, j, h_codes, h_scales, h_weight, g, False, g == PASSES - 1)
 
         def gate_value(bank, gate, j):
             value = work.tile([P, N_TILE], F32, tag="gate")
@@ -196,10 +213,11 @@ def tile_naivelstm_pb_kernel(
             nc.scalar.activation(out=value[:], in_=value[:], func=SIGMOID)
             return value
 
-        f_banks = gate_sums("f", "if", "hf")
+        f_banks = open_banks("f", "if", "hf")
         c_next = keep.tile([P, FEATURES], F32)
         tanh_c = keep.tile([P, FEATURES], F32)
         for j in range(CHUNKS):
+            close_bank(f_banks[j], j, "hf")
             f_gate = gate_value(f_banks[j], 0, j)
             nc.vector.tensor_tensor(out=c_next[:, chunk(j)], in0=f_gate[:], in1=c_sb[:, chunk(j)], op=MULT)
             nc.vector.tensor_tensor(
@@ -208,8 +226,9 @@ def tile_naivelstm_pb_kernel(
             nc.scalar.activation(out=tanh_c[:, chunk(j)], in_=c_next[:, chunk(j)], func=TANH)
         nc.sync.dma_start(out=out_1, in_=c_next[:])
 
-        o_banks = gate_sums("o", "io", "ho")
+        o_banks = open_banks("o", "io", "ho")
         for j in range(CHUNKS):
+            close_bank(o_banks[j], j, "ho")
             o_gate = gate_value(o_banks[j], 1, j)
             h_next = result.tile([P, N_TILE], F32)
             nc.vector.tensor_tensor(out=h_next[:], in0=o_gate[:], in1=tanh_c[:, chunk(j)], op=MULT)

@@ -80,6 +80,7 @@ def tile_naivelstm_pb_kernel(
         tc.tile_pool(name="work", bufs=3) as work,
         tc.tile_pool(name="result", bufs=CHUNKS) as result,
         tc.psum_pool(name="psum", bufs=8) as psum,
+        tc.manual_schedule(),
     ):
         planes = {}
         for name in ("if", "hf", "io", "ho"):
@@ -213,23 +214,42 @@ def tile_naivelstm_pb_kernel(
             nc.scalar.activation(out=value[:], in_=value[:], func=SIGMOID)
             return value
 
+        def one_bank_behind(first_half, second_half):
+            for j in range(CHUNKS + 1):
+                if j < CHUNKS:
+                    first_half(j)
+                if j > 0:
+                    second_half(j - 1)
+
         f_banks = open_banks("f", "if", "hf")
+        f_gate = {}
         c_next = keep.tile([P, FEATURES], F32)
         tanh_c = keep.tile([P, FEATURES], F32)
-        for j in range(CHUNKS):
+
+        def forget_gate(j):
             close_bank(f_banks[j], j, "hf")
-            f_gate = gate_value(f_banks[j], 0, j)
-            nc.vector.tensor_tensor(out=c_next[:, chunk(j)], in0=f_gate[:], in1=c_sb[:, chunk(j)], op=MULT)
+            f_gate[j] = gate_value(f_banks[j], 0, j)
+
+        def cell_state(j):
+            nc.vector.tensor_tensor(out=c_next[:, chunk(j)], in0=f_gate[j][:], in1=c_sb[:, chunk(j)], op=MULT)
             nc.vector.tensor_tensor(
                 out=c_next[:, chunk(j)], in0=c_next[:, chunk(j)], in1=ig_rows[:, chunk(j)], op=ADD
             )
             nc.scalar.activation(out=tanh_c[:, chunk(j)], in_=c_next[:, chunk(j)], func=TANH)
+
+        one_bank_behind(forget_gate, cell_state)
         nc.sync.dma_start(out=out_1, in_=c_next[:])
 
         o_banks = open_banks("o", "io", "ho")
-        for j in range(CHUNKS):
+        o_gate = {}
+
+        def output_gate(j):
             close_bank(o_banks[j], j, "ho")
-            o_gate = gate_value(o_banks[j], 1, j)
+            o_gate[j] = gate_value(o_banks[j], 1, j)
+
+        def hidden_state(j):
             h_next = result.tile([P, N_TILE], F32)
-            nc.vector.tensor_tensor(out=h_next[:], in0=o_gate[:], in1=tanh_c[:, chunk(j)], op=MULT)
+            nc.vector.tensor_tensor(out=h_next[:], in0=o_gate[j][:], in1=tanh_c[:, chunk(j)], op=MULT)
             nc.sync.dma_start(out=out_0[:, chunk(j)], in_=h_next[:])
+
+        one_bank_behind(output_gate, hidden_state)

@@ -82,12 +82,13 @@ def tile_naivelstm_pb_kernel(
         tc.psum_pool(name="psum", bufs=8) as psum,
         tc.manual_schedule(),
     ):
+        bias_rows = keep.tile([P, 2, FEATURES], BF16)
         planes = {}
         for name in ("if", "hf", "io", "ho"):
             planes[name] = keep.tile([P, FEATURES], U8, name="%s_planes" % name, align_bytes=64)
             nc.vector.memset(planes[name][:].bitcast(I32), 0)
-        bias_rows = keep.tile([P, 2, FEATURES], BF16)
-        nc.vector.memset(bias_rows[:], 0.0)
+            if name == "if":
+                nc.vector.memset(bias_rows[:].rearrange("p g n -> p (g n)").bitcast(I32), 0)
         ones = keep.tile([P, P], BF16)
         nc.vector.memset(ones[:], 1.0)
         ident_f32 = keep.tile([P, P], F32)
@@ -99,9 +100,6 @@ def tile_naivelstm_pb_kernel(
         nc.sync.dma_start(out=x_raw[:], in_=x.rearrange("(g p t) b -> p g t b", p=P, t=PACK))
         h_raw = keep.tile([P, FEATURES], BF16)
         nc.sync.dma_start(out=h_raw[:], in_=h)
-        for gate, (b_x, b_h) in enumerate(((b_if, b_hf), (b_io, b_ho))):
-            nc.scalar.dma_start(out=bias_rows[0:1, gate, :], in_=b_x.rearrange("n o -> o n"))
-            nc.scalar.dma_start(out=bias_rows[1:2, gate, :], in_=b_h.rearrange("n o -> o n"))
         ig_raw = keep.tile([P, CHUNKS, PACK, P], BF16)
         nc.sync.dma_start(out=ig_raw[:], in_=ig.rearrange("(j p t) b -> p j t b", p=P, t=PACK))
         load_scale_planes(nc, planes["if"], w_if_scales)
@@ -110,6 +108,9 @@ def tile_naivelstm_pb_kernel(
         load_scale_planes(nc, planes["ho"], w_ho_scales)
         c_sb = keep.tile([P, FEATURES], BF16)
         nc.sync.dma_start(out=c_sb[:], in_=c)
+        for gate, (b_x, b_h) in enumerate(((b_if, b_hf), (b_io, b_ho))):
+            nc.scalar.dma_start(out=bias_rows[0:1, gate, :], in_=b_x.rearrange("n o -> o n"))
+            nc.scalar.dma_start(out=bias_rows[1:2, gate, :], in_=b_h.rearrange("n o -> o n"))
         words = {}
         for name in ("if", "hf", "io", "ho"):
             words[name] = words_tiles(keep, name)

@@ -23,6 +23,8 @@ QUADRANT = 32
 ROWS = 4
 LATE_PASSES = 2
 
+ALIGN = 256
+
 FLOPS = 4 * 2 * FEATURES * FEATURES * P
 
 
@@ -32,7 +34,7 @@ def chunk(j):
 
 def words_tiles(pool, name):
     return [
-        pool.tile([P, FEATURES], U32, name="%s_words_%d" % (name, g), align_bytes=64)
+        pool.tile([P, FEATURES], U32, name="%s_words_%d" % (name, g), align_bytes=ALIGN)
         for g in range(PASSES)
     ]
 
@@ -82,10 +84,10 @@ def tile_naivelstm_pb_kernel(
         tc.psum_pool(name="psum", bufs=8) as psum,
         tc.manual_schedule(),
     ):
-        bias_rows = keep.tile([P, 2, FEATURES], BF16)
+        bias_rows = keep.tile([P, 2, FEATURES], BF16, align_bytes=ALIGN)
         planes = {}
         for name in ("if", "hf", "io", "ho"):
-            planes[name] = keep.tile([P, FEATURES], U8, name="%s_planes" % name, align_bytes=64)
+            planes[name] = keep.tile([P, FEATURES], U8, name="%s_planes" % name, align_bytes=ALIGN)
             nc.vector.memset(planes[name][:].bitcast(I32), 0)
             if name == "if":
                 nc.vector.memset(bias_rows[:].rearrange("p g n -> p (g n)").bitcast(I32), 0)
@@ -96,17 +98,17 @@ def tile_naivelstm_pb_kernel(
         ident_bf16 = keep.tile([P, P], BF16)
         make_identity(nc, ident_bf16[:])
 
-        x_raw = keep.tile([P, PASSES, PACK, P], BF16)
+        x_raw = keep.tile([P, PASSES, PACK, P], BF16, align_bytes=ALIGN)
         nc.sync.dma_start(out=x_raw[:], in_=x.rearrange("(g p t) b -> p g t b", p=P, t=PACK))
-        h_raw = keep.tile([P, FEATURES], BF16)
+        h_raw = keep.tile([P, FEATURES], BF16, align_bytes=ALIGN)
         nc.sync.dma_start(out=h_raw[:], in_=h)
-        ig_raw = keep.tile([P, CHUNKS, PACK, P], BF16)
+        ig_raw = keep.tile([P, CHUNKS, PACK, P], BF16, align_bytes=ALIGN)
         nc.sync.dma_start(out=ig_raw[:], in_=ig.rearrange("(j p t) b -> p j t b", p=P, t=PACK))
         load_scale_planes(nc, planes["if"], w_if_scales)
         load_scale_planes(nc, planes["hf"], w_hf_scales)
         load_scale_planes(nc, planes["io"], w_io_scales)
         load_scale_planes(nc, planes["ho"], w_ho_scales)
-        c_sb = keep.tile([P, FEATURES], BF16)
+        c_sb = keep.tile([P, FEATURES], BF16, align_bytes=ALIGN)
         nc.sync.dma_start(out=c_sb[:], in_=c)
         for gate, (b_x, b_h) in enumerate(((b_if, b_hf), (b_io, b_ho))):
             nc.scalar.dma_start(out=bias_rows[0:1, gate, :], in_=b_x.rearrange("n o -> o n"))
@@ -123,10 +125,10 @@ def tile_naivelstm_pb_kernel(
             for g in range(PASSES - LATE_PASSES, PASSES):
                 load_words(nc, words["ho"][g], w_ho_words[g], chunk(j))
 
-        x_grouped = keep.tile([P, PASSES, P, PACK], BF16, align_bytes=64)
+        x_grouped = keep.tile([P, PASSES, P, PACK], BF16, align_bytes=ALIGN)
         nc.vector.tensor_copy(out=x_grouped[:], in_=x_raw[:].rearrange("p g t b -> p g b t"))
-        x_codes = keep.tile([P, PASSES, P], U32, align_bytes=64)
-        x_scales = keep.tile([P, PASSES, P], U8, align_bytes=64)
+        x_codes = keep.tile([P, PASSES, P], U32, align_bytes=ALIGN)
+        x_scales = keep.tile([P, PASSES, P], U8, align_bytes=ALIGN)
         nc.vector.quantize_mx(
             out=x_codes[:].rearrange("p g b -> p (g b)").bitcast(FP8X4),
             scales=x_scales[:].rearrange("p g b -> p (g b)"),
@@ -134,7 +136,7 @@ def tile_naivelstm_pb_kernel(
         )
 
         h_words = h_raw[:].bitcast(F32)
-        h_grouped = keep.tile([P, PASSES, P, 2], F32, align_bytes=64)
+        h_grouped = keep.tile([P, PASSES, P, 2], F32, align_bytes=ALIGN)
         for half in range(2):
             h_t = psum.tile([P, 2, 2, P], F32, tag="bank")
             for gg in range(2):
@@ -149,8 +151,8 @@ def tile_naivelstm_pb_kernel(
                 out=h_grouped[:, 2 * half : 2 * half + 2, :, :],
                 in_=h_t[:].rearrange("p g u b -> p g b u"),
             )
-        h_codes = keep.tile([P, PASSES, P], U32, align_bytes=64)
-        h_scales = keep.tile([P, PASSES, P], U8, align_bytes=64)
+        h_codes = keep.tile([P, PASSES, P], U32, align_bytes=ALIGN)
+        h_scales = keep.tile([P, PASSES, P], U8, align_bytes=ALIGN)
         nc.vector.quantize_mx(
             out=h_codes[:].rearrange("p g b -> p (g b)").bitcast(FP8X4),
             scales=h_scales[:].rearrange("p g b -> p (g b)"),
@@ -224,8 +226,8 @@ def tile_naivelstm_pb_kernel(
 
         f_banks = open_banks("f", "if", "hf")
         f_gate = {}
-        c_next = keep.tile([P, FEATURES], F32)
-        tanh_c = keep.tile([P, FEATURES], F32)
+        c_next = keep.tile([P, FEATURES], F32, align_bytes=ALIGN)
+        tanh_c = keep.tile([P, FEATURES], F32, align_bytes=ALIGN)
 
         def forget_gate(j):
             close_bank(f_banks[j], j, "hf")
@@ -249,7 +251,7 @@ def tile_naivelstm_pb_kernel(
             o_gate[j] = gate_value(o_banks[j], 1, j)
 
         def hidden_state(j):
-            h_next = result.tile([P, N_TILE], F32)
+            h_next = result.tile([P, N_TILE], F32, align_bytes=ALIGN)
             nc.vector.tensor_tensor(out=h_next[:], in0=o_gate[j][:], in1=tanh_c[:, chunk(j)], op=MULT)
             nc.sync.dma_start(out=out_0[:, chunk(j)], in_=h_next[:])
 

@@ -19,6 +19,9 @@ FEATURES = 2048
 PASSES = FEATURES // K_PASS
 N_TILE = 512
 CHUNKS = FEATURES // N_TILE
+BANKS = [slice(j * N_TILE, (j + 1) * N_TILE) for j in range(CHUNKS)]
+HALF = N_TILE // 2
+FINE_BANKS = BANKS[:-1] + [slice(FEATURES - N_TILE, FEATURES - HALF), slice(FEATURES - HALF, FEATURES)]
 QUADRANT = 32
 ROWS = 4
 LATE_PASSES = 2
@@ -26,10 +29,6 @@ LATE_PASSES = 2
 ALIGN = 256
 
 FLOPS = 4 * 2 * FEATURES * FEATURES * P
-
-
-def chunk(j):
-    return slice(j * N_TILE, (j + 1) * N_TILE)
 
 
 def words_tiles(pool, name):
@@ -80,7 +79,7 @@ def tile_naivelstm_pb_kernel(
     with (
         tc.tile_pool(name="keep", bufs=1) as keep,
         tc.tile_pool(name="work", bufs=3) as work,
-        tc.tile_pool(name="result", bufs=CHUNKS) as result,
+        tc.tile_pool(name="result", bufs=len(FINE_BANKS)) as result,
         tc.psum_pool(name="psum", bufs=8) as psum,
         tc.manual_schedule(),
     ):
@@ -121,9 +120,9 @@ def tile_naivelstm_pb_kernel(
                 load_words(nc, words[name][g], dram[g], slice(0, FEATURES))
         for g in range(PASSES - LATE_PASSES):
             load_words(nc, words["ho"][g], w_ho_words[g], slice(0, FEATURES))
-        for j in range(CHUNKS):
+        for columns in FINE_BANKS:
             for g in range(PASSES - LATE_PASSES, PASSES):
-                load_words(nc, words["ho"][g], w_ho_words[g], chunk(j))
+                load_words(nc, words["ho"][g], w_ho_words[g], columns)
 
         x_grouped = keep.tile([P, PASSES, P, PACK], BF16, align_bytes=ALIGN)
         nc.vector.tensor_copy(out=x_grouped[:], in_=x_raw[:].rearrange("p g t b -> p g b t"))
@@ -175,84 +174,86 @@ def tile_naivelstm_pb_kernel(
 
         bias_all = keep.tile([P, 2, FEATURES], F32)
         for gate in range(2):
-            for j in range(CHUNKS):
+            for columns in BANKS:
                 bias_bank = psum.tile([P, N_TILE], F32, tag="bank")
                 nc.tensor.matmul(
-                    out=bias_bank[:], lhsT=ones[:], rhs=bias_rows[:, gate, chunk(j)],
+                    out=bias_bank[:], lhsT=ones[:], rhs=bias_rows[:, gate, columns],
                     start=True, stop=True,
                 )
-                nc.scalar.copy(out=bias_all[:, gate, chunk(j)], in_=bias_bank[:])
+                nc.scalar.copy(out=bias_all[:, gate, columns], in_=bias_bank[:])
 
-        def mx_pass(bank, j, codes, scales, weight, g, start, stop):
+        def mx_pass(bank, columns, codes, scales, weight, g, start, stop):
             nc.tensor.matmul_mx(
-                out=bank[:],
+                out=bank,
                 lhsT=codes[:, g, :].bitcast(FP8X4),
                 lhsT_scale=scales[:, g, :],
-                rhs=words[weight][g][:, chunk(j)].bitcast(FP8X4),
-                rhs_scale=planes[weight][ROWS * g : P, chunk(j)],
+                rhs=words[weight][g][:, columns].bitcast(FP8X4),
+                rhs_scale=planes[weight][ROWS * g : P, columns],
                 start=start,
                 stop=stop,
             )
 
-        def open_banks(gate_name, x_weight, h_weight):
-            banks = [
-                psum.tile([P, N_TILE], F32, tag="bank", name="%s_bank_%d" % (gate_name, j))
-                for j in range(CHUNKS)
-            ]
+        def open_banks(gate_name, cuts, x_weight, h_weight):
+            banks = []
+            for j, columns in enumerate(cuts):
+                bank = psum.tile([P, N_TILE], F32, tag="bank", name="%s_bank_%d" % (gate_name, j))
+                banks.append(bank[:, : columns.stop - columns.start])
             for g in range(PASSES):
-                for j in range(CHUNKS):
-                    mx_pass(banks[j], j, x_codes, x_scales, x_weight, g, g == 0, False)
+                for bank, columns in zip(banks, cuts):
+                    mx_pass(bank, columns, x_codes, x_scales, x_weight, g, g == 0, False)
             for g in range(PASSES - LATE_PASSES):
-                for j in range(CHUNKS):
-                    mx_pass(banks[j], j, h_codes, h_scales, h_weight, g, False, False)
+                for bank, columns in zip(banks, cuts):
+                    mx_pass(bank, columns, h_codes, h_scales, h_weight, g, False, False)
             return banks
 
-        def close_bank(bank, j, h_weight):
+        def close_bank(bank, columns, h_weight):
             for g in range(PASSES - LATE_PASSES, PASSES):
-                mx_pass(bank, j, h_codes, h_scales, h_weight, g, False, g == PASSES - 1)
+                mx_pass(bank, columns, h_codes, h_scales, h_weight, g, False, g == PASSES - 1)
 
-        def gate_value(bank, gate, j):
-            value = work.tile([P, N_TILE], F32, tag="gate")
-            nc.vector.tensor_tensor(out=value[:], in0=bank[:], in1=bias_all[:, gate, chunk(j)], op=ADD)
-            nc.scalar.activation(out=value[:], in_=value[:], func=SIGMOID)
+        def gate_value(bank, gate, columns):
+            tile = work.tile([P, N_TILE], F32, tag="gate")
+            value = tile[:, : columns.stop - columns.start]
+            nc.vector.tensor_tensor(out=value, in0=bank, in1=bias_all[:, gate, columns], op=ADD)
+            nc.scalar.activation(out=value, in_=value, func=SIGMOID)
             return value
 
-        def one_bank_behind(first_half, second_half):
-            for j in range(CHUNKS + 1):
-                if j < CHUNKS:
-                    first_half(j)
+        def one_bank_behind(first_half, second_half, cuts):
+            for j in range(len(cuts) + 1):
+                if j < len(cuts):
+                    first_half(j, cuts[j])
                 if j > 0:
-                    second_half(j - 1)
+                    second_half(j - 1, cuts[j - 1])
 
-        f_banks = open_banks("f", "if", "hf")
+        f_banks = open_banks("f", BANKS, "if", "hf")
         f_gate = {}
         c_next = keep.tile([P, FEATURES], F32, align_bytes=ALIGN)
         tanh_c = keep.tile([P, FEATURES], F32, align_bytes=ALIGN)
 
-        def forget_gate(j):
-            close_bank(f_banks[j], j, "hf")
-            f_gate[j] = gate_value(f_banks[j], 0, j)
+        def forget_gate(j, columns):
+            close_bank(f_banks[j], columns, "hf")
+            f_gate[j] = gate_value(f_banks[j], 0, columns)
 
-        def cell_state(j):
-            nc.vector.tensor_tensor(out=c_next[:, chunk(j)], in0=f_gate[j][:], in1=c_sb[:, chunk(j)], op=MULT)
+        def cell_state(j, columns):
+            nc.vector.tensor_tensor(out=c_next[:, columns], in0=f_gate[j], in1=c_sb[:, columns], op=MULT)
             nc.vector.tensor_tensor(
-                out=c_next[:, chunk(j)], in0=c_next[:, chunk(j)], in1=ig_rows[:, chunk(j)], op=ADD
+                out=c_next[:, columns], in0=c_next[:, columns], in1=ig_rows[:, columns], op=ADD
             )
-            nc.scalar.activation(out=tanh_c[:, chunk(j)], in_=c_next[:, chunk(j)], func=TANH)
+            nc.scalar.activation(out=tanh_c[:, columns], in_=c_next[:, columns], func=TANH)
 
-        one_bank_behind(forget_gate, cell_state)
+        one_bank_behind(forget_gate, cell_state, BANKS)
         nc.sync.dma_start(out=out_1, in_=c_next[:])
 
-        o_banks = open_banks("o", "io", "ho")
+        o_banks = open_banks("o", FINE_BANKS, "io", "ho")
         o_gate = {}
 
-        def output_gate(j):
-            close_bank(o_banks[j], j, "ho")
-            o_gate[j] = gate_value(o_banks[j], 1, j)
+        def output_gate(j, columns):
+            close_bank(o_banks[j], columns, "ho")
+            o_gate[j] = gate_value(o_banks[j], 1, columns)
 
-        def hidden_state(j):
-            h_next = result.tile([P, N_TILE], F32, align_bytes=ALIGN)
-            nc.vector.tensor_tensor(out=h_next[:], in0=o_gate[j][:], in1=tanh_c[:, chunk(j)], op=MULT)
-            nc.sync.dma_start(out=out_0[:, chunk(j)], in_=h_next[:])
+        def hidden_state(j, columns):
+            tile = result.tile([P, N_TILE], F32, align_bytes=ALIGN)
+            h_next = tile[:, : columns.stop - columns.start]
+            nc.vector.tensor_tensor(out=h_next, in0=o_gate[j], in1=tanh_c[:, columns], op=MULT)
+            nc.sync.dma_start(out=out_0[:, columns], in_=h_next)
 
-        one_bank_behind(output_gate, hidden_state)
+        one_bank_behind(output_gate, hidden_state, FINE_BANKS)

@@ -24,6 +24,7 @@ HALF = N_TILE // 2
 FINE_BANKS = BANKS[:-1] + [slice(FEATURES - N_TILE, FEATURES - HALF), slice(FEATURES - HALF, FEATURES)]
 QUADRANT = 32
 ROWS = 4
+SLIVER = 64
 LATE_PASSES = 2
 
 ALIGN = 256
@@ -46,12 +47,13 @@ def load_words(nc, tile_g, words_g, columns):
 
 
 def load_scale_planes(nc, planes, scales):
-    for quadrant in range(P // QUADRANT):
+    for quadrant in (0, 2, 1, 3):
         first = quadrant * QUADRANT
-        nc.gpsimd.dma_start(
-            out=planes[first : first + PASSES * ROWS, :].bitcast(F32),
-            in_=scales[:, quadrant * ROWS : (quadrant + 1) * ROWS, :].bitcast(F32),
-        )
+        for columns in (slice(0, FEATURES - SLIVER), slice(FEATURES - SLIVER, FEATURES)):
+            nc.gpsimd.dma_start(
+                out=planes[first : first + PASSES * ROWS, columns].bitcast(F32),
+                in_=scales[:, quadrant * ROWS : (quadrant + 1) * ROWS, columns].bitcast(F32),
+            )
 
 
 def tile_naivelstm_pb_kernel(

import concourse.mybir as mybir
from concourse.masks import make_identity

F32 = mybir.dt.float32
BF16 = mybir.dt.bfloat16
I32 = mybir.dt.int32
U32 = mybir.dt.uint32
U8 = mybir.dt.uint8
FP8X4 = mybir.dt.float8_e4m3fn_x4
ADD = mybir.AluOpType.add
MULT = mybir.AluOpType.mult
SIGMOID = mybir.ActivationFunctionType.Sigmoid
TANH = mybir.ActivationFunctionType.Tanh

P = 128
PACK = 4
K_PASS = P * PACK
FEATURES = 2048
PASSES = FEATURES // K_PASS
N_TILE = 512
CHUNKS = FEATURES // N_TILE
BANKS = [slice(j * N_TILE, (j + 1) * N_TILE) for j in range(CHUNKS)]
HALF = N_TILE // 2
FINE_BANKS = BANKS[:-1] + [slice(FEATURES - N_TILE, FEATURES - HALF), slice(FEATURES - HALF, FEATURES)]
QUADRANT = 32
ROWS = 4
SLIVER = 64
LATE_PASSES = 2

ALIGN = 256

FLOPS = 4 * 2 * FEATURES * FEATURES * P


def words_tiles(pool, name):
    return [
        pool.tile([P, FEATURES], U32, name="%s_words_%d" % (name, g), align_bytes=ALIGN)
        for g in range(PASSES)
    ]


def load_words(nc, tile_g, words_g, columns):
    nc.sync.dma_start(
        out=tile_g[:, columns].bitcast(I32),
        in_=words_g.rearrange("p n t -> p (n t)").bitcast(I32)[:, columns],
    )


def load_scale_planes(nc, planes, scales):
    for quadrant in (0, 2, 1, 3):
        first = quadrant * QUADRANT
        for columns in (slice(0, FEATURES - SLIVER), slice(FEATURES - SLIVER, FEATURES)):
            nc.gpsimd.dma_start(
                out=planes[first : first + PASSES * ROWS, columns].bitcast(F32),
                in_=scales[:, quadrant * ROWS : (quadrant + 1) * ROWS, columns].bitcast(F32),
            )


def tile_naivelstm_pb_kernel(
    tc,
    x,
    h,
    c,
    ig,
    w_if_words,
    w_if_scales,
    w_io_words,
    w_io_scales,
    w_hf_words,
    w_hf_scales,
    w_ho_words,
    w_ho_scales,
    b_if,
    b_hf,
    b_io,
    b_ho,
    out_0,
    out_1,
):
    nc = tc.nc
    with (
        tc.tile_pool(name="keep", bufs=1) as keep,
        tc.tile_pool(name="work", bufs=3) as work,
        tc.tile_pool(name="result", bufs=len(FINE_BANKS)) as result,
        tc.psum_pool(name="psum", bufs=8) as psum,
        tc.manual_schedule(),
    ):
        bias_rows = keep.tile([P, 2, FEATURES], BF16, align_bytes=ALIGN)
        planes = {}
        for name in ("if", "hf", "io", "ho"):
            planes[name] = keep.tile([P, FEATURES], U8, name="%s_planes" % name, align_bytes=ALIGN)
            nc.vector.memset(planes[name][:].bitcast(I32), 0)
            if name == "if":
                nc.vector.memset(bias_rows[:].rearrange("p g n -> p (g n)").bitcast(I32), 0)
        ones = keep.tile([P, P], BF16)
        nc.vector.memset(ones[:], 1.0)
        ident_f32 = keep.tile([P, P], F32)
        make_identity(nc, ident_f32[:])
        ident_bf16 = keep.tile([P, P], BF16)
        make_identity(nc, ident_bf16[:])

        x_raw = keep.tile([P, PASSES, PACK, P], BF16, align_bytes=ALIGN)
        nc.sync.dma_start(out=x_raw[:], in_=x.rearrange("(g p t) b -> p g t b", p=P, t=PACK))
        h_raw = keep.tile([P, FEATURES], BF16, align_bytes=ALIGN)
        nc.sync.dma_start(out=h_raw[:], in_=h)
        ig_raw = keep.tile([P, CHUNKS, PACK, P], BF16, align_bytes=ALIGN)
        nc.sync.dma_start(out=ig_raw[:], in_=ig.rearrange("(j p t) b -> p j t b", p=P, t=PACK))
        load_scale_planes(nc, planes["if"], w_if_scales)
        load_scale_planes(nc, planes["hf"], w_hf_scales)
        load_scale_planes(nc, planes["io"], w_io_scales)
        load_scale_planes(nc, planes["ho"], w_ho_scales)
        c_sb = keep.tile([P, FEATURES], BF16, align_bytes=ALIGN)
        nc.sync.dma_start(out=c_sb[:], in_=c)
        for gate, (b_x, b_h) in enumerate(((b_if, b_hf), (b_io, b_ho))):
            nc.scalar.dma_start(out=bias_rows[0:1, gate, :], in_=b_x.rearrange("n o -> o n"))
            nc.scalar.dma_start(out=bias_rows[1:2, gate, :], in_=b_h.rearrange("n o -> o n"))
        words = {}
        for name in ("if", "hf", "io", "ho"):
            words[name] = words_tiles(keep, name)
        for name, dram in (("if", w_if_words), ("hf", w_hf_words), ("io", w_io_words)):
            for g in range(PASSES):
                load_words(nc, words[name][g], dram[g], slice(0, FEATURES))
        for g in range(PASSES - LATE_PASSES):
            load_words(nc, words["ho"][g], w_ho_words[g], slice(0, FEATURES))
        for columns in FINE_BANKS:
            for g in range(PASSES - LATE_PASSES, PASSES):
                load_words(nc, words["ho"][g], w_ho_words[g], columns)

        x_grouped = keep.tile([P, PASSES, P, PACK], BF16, align_bytes=ALIGN)
        nc.vector.tensor_copy(out=x_grouped[:], in_=x_raw[:].rearrange("p g t b -> p g b t"))
        x_codes = keep.tile([P, PASSES, P], U32, align_bytes=ALIGN)
        x_scales = keep.tile([P, PASSES, P], U8, align_bytes=ALIGN)
        nc.vector.quantize_mx(
            out=x_codes[:].rearrange("p g b -> p (g b)").bitcast(FP8X4),
            scales=x_scales[:].rearrange("p g b -> p (g b)"),
            in_=x_grouped[:].rearrange("p g b t -> p (g b t)"),
        )

        h_words = h_raw[:].bitcast(F32)
        h_grouped = keep.tile([P, PASSES, P, 2], F32, align_bytes=ALIGN)
        for half in range(2):
            h_t = psum.tile([P, 2, 2, P], F32, tag="bank")
            for gg in range(2):
                g = 2 * half + gg
                for u in range(2):
                    nc.tensor.transpose(
                        h_t[:, gg, u, :],
                        h_words[:, 256 * g + u : 256 * (g + 1) : 2],
                        ident_f32[:],
                    )
            nc.vector.tensor_copy(
                out=h_grouped[:, 2 * half : 2 * half + 2, :, :],
                in_=h_t[:].rearrange("p g u b -> p g b u"),
            )
        h_codes = keep.tile([P, PASSES, P], U32, align_bytes=ALIGN)
        h_scales = keep.tile([P, PASSES, P], U8, align_bytes=ALIGN)
        nc.vector.quantize_mx(
            out=h_codes[:].rearrange("p g b -> p (g b)").bitcast(FP8X4),
            scales=h_scales[:].rearrange("p g b -> p (g b)"),
            in_=h_grouped[:].rearrange("p g b u -> p (g b u)").bitcast(BF16),
        )

        ig_t = keep.tile([P, CHUNKS, P, PACK], BF16)
        for half in range(2):
            ig_bank = psum.tile([P, 2, PACK, P], BF16, tag="bank")
            for jj in range(2):
                for t in range(PACK):
                    nc.tensor.transpose(
                        ig_bank[:, jj, t, :], ig_raw[:, 2 * half + jj, t, :], ident_bf16[:]
                    )
            nc.vector.tensor_copy(
                out=ig_t[:, 2 * half : 2 * half + 2, :, :],
                in_=ig_bank[:].rearrange("b j t p -> b j p t"),
            )
        ig_rows = ig_t[:].rearrange("b j p t -> b (j p t)")

        bias_all = keep.tile([P, 2, FEATURES], F32)
        for gate in range(2):
            for columns in BANKS:
                bias_bank = psum.tile([P, N_TILE], F32, tag="bank")
                nc.tensor.matmul(
                    out=bias_bank[:], lhsT=ones[:], rhs=bias_rows[:, gate, columns],
                    start=True, stop=True,
                )
                nc.scalar.copy(out=bias_all[:, gate, columns], in_=bias_bank[:])

        def mx_pass(bank, columns, codes, scales, weight, g, start, stop):
            nc.tensor.matmul_mx(
                out=bank,
                lhsT=codes[:, g, :].bitcast(FP8X4),
                lhsT_scale=scales[:, g, :],
                rhs=words[weight][g][:, columns].bitcast(FP8X4),
                rhs_scale=planes[weight][ROWS * g : P, columns],
                start=start,
                stop=stop,
            )

        def open_banks(gate_name, cuts, x_weight, h_weight):
            banks = []
            for j, columns in enumerate(cuts):
                bank = psum.tile([P, N_TILE], F32, tag="bank", name="%s_bank_%d" % (gate_name, j))
                banks.append(bank[:, : columns.stop - columns.start])
            for g in range(PASSES):
                for bank, columns in zip(banks, cuts):
                    mx_pass(bank, columns, x_codes, x_scales, x_weight, g, g == 0, False)
            for g in range(PASSES - LATE_PASSES):
                for bank, columns in zip(banks, cuts):
                    mx_pass(bank, columns, h_codes, h_scales, h_weight, g, False, False)
            return banks

        def close_bank(bank, columns, h_weight):
            for g in range(PASSES - LATE_PASSES, PASSES):
                mx_pass(bank, columns, h_codes, h_scales, h_weight, g, False, g == PASSES - 1)

        def gate_value(bank, gate, columns):
            tile = work.tile([P, N_TILE], F32, tag="gate")
            value = tile[:, : columns.stop - columns.start]
            nc.vector.tensor_tensor(out=value, in0=bank, in1=bias_all[:, gate, columns], op=ADD)
            nc.scalar.activation(out=value, in_=value, func=SIGMOID)
            return value

        def one_bank_behind(first_half, second_half, cuts):
            for j in range(len(cuts) + 1):
                if j < len(cuts):
                    first_half(j, cuts[j])
                if j > 0:
                    second_half(j - 1, cuts[j - 1])

        f_banks = open_banks("f", BANKS, "if", "hf")
        f_gate = {}
        c_next = keep.tile([P, FEATURES], F32, align_bytes=ALIGN)
        tanh_c = keep.tile([P, FEATURES], F32, align_bytes=ALIGN)

        def forget_gate(j, columns):
            close_bank(f_banks[j], columns, "hf")
            f_gate[j] = gate_value(f_banks[j], 0, columns)

        def cell_state(j, columns):
            nc.vector.tensor_tensor(out=c_next[:, columns], in0=f_gate[j], in1=c_sb[:, columns], op=MULT)
            nc.vector.tensor_tensor(
                out=c_next[:, columns], in0=c_next[:, columns], in1=ig_rows[:, columns], op=ADD
            )
            nc.scalar.activation(out=tanh_c[:, columns], in_=c_next[:, columns], func=TANH)

        one_bank_behind(forget_gate, cell_state, BANKS)
        nc.sync.dma_start(out=out_1, in_=c_next[:])

        o_banks = open_banks("o", FINE_BANKS, "io", "ho")
        o_gate = {}

        def output_gate(j, columns):
            close_bank(o_banks[j], columns, "ho")
            o_gate[j] = gate_value(o_banks[j], 1, columns)

        def hidden_state(j, columns):
            tile = result.tile([P, N_TILE], F32, align_bytes=ALIGN)
            h_next = tile[:, : columns.stop - columns.start]
            nc.vector.tensor_tensor(out=h_next, in0=o_gate[j], in1=tanh_c[:, columns], op=MULT)
            nc.sync.dma_start(out=out_0[:, columns], in_=h_next)

        one_bank_behind(output_gate, hidden_state, FINE_BANKS)
